import numpy as np
import ml_dtypes


def mxq(x, axis, fmt="e4m3"):
    dtype, down = {"e4m3": (ml_dtypes.float8_e4m3fn, 7), "e5m2": (ml_dtypes.float8_e5m2, 14)}[fmt]
    v = np.moveaxis(np.asarray(x, np.float32).astype(ml_dtypes.bfloat16).astype(np.float64), axis, -1)
    blocks = v.reshape(v.shape[:-1] + (-1, 32))
    amax = np.abs(blocks).max(-1, keepdims=True)
    byte = np.maximum(np.where(amax > 0, np.frexp(amax)[1] - 1 + 127, 0) - down, 1)
    scale = np.exp2(byte - 127.0)
    codes = (blocks / scale).astype(np.float32).astype(dtype).astype(np.float64)
    return np.moveaxis((codes * scale).reshape(v.shape), -1, axis)


WIDE = False


def mx_kscale(k):
    if not WIDE:
        return np.ones(k)
    levels = np.array([10, -10, 5, -5, 0])
    a = np.random.permutation(np.resize(levels, k // 512 * 4)).reshape(k // 512, 4)
    idx = np.arange(k)
    return np.exp2(a[idx // 512, idx % 128 // 32])


BF16 = ml_dtypes.bfloat16


def bf(x):
    return np.asarray(x, np.float32).astype(BF16)


def f64(x):
    return np.asarray(x).astype(np.float64)


B, T, C, CO, HS, DW, DA, DV, DG = 4, 1024, 1024, 256, 64, 128, 128, 128, 256
H = CO // HS
EPS_NORM = 1e-12


def sigmoid(u):
    return 1.0 / (1.0 + np.exp(-u))


def setup_inputs():
    n = np.random.standard_normal
    s = mx_kscale(C)
    return {
        "x": bf(n((B, T, C)) * s),
        "x_k": bf(n((1, 1, C)) * 0.3),
        "W_k": bf(n((CO, C)) / np.sqrt(C) / s),
        "a_hid": bf(n((B, T, DA))),
        "a2": bf(n((DA, CO)) / np.sqrt(DA)),
        "a0": bf(n((1, 1, CO)) * 0.5),
        "k_k": bf(0.71 + n((1, 1, CO)) * 0.2),
        "k_a": bf(1.02 + n((1, 1, CO)) * 0.2),
    }


def reference(x, x_k, W_k, a_hid, a2, a0, k_k, k_a):
    x = f64(x)
    prev = np.concatenate([np.zeros_like(x[:, :1]), x[:, :-1]], axis=1)
    xk = x + (prev - x) * f64(x_k)
    k = mxq(xk, 2, "e4m3") @ mxq(f64(W_k), 1, "e4m3").T
    a = sigmoid(f64(a0) + f64(a_hid) @ f64(a2))
    kkh = (k * f64(k_k)).reshape(B, T, H, HS)
    nrm = np.sqrt(np.sum(kkh * kkh, axis=-1, keepdims=True))
    kk = (kkh / np.maximum(nrm, EPS_NORM)).reshape(B, T, CO)
    k_out = k * (1.0 + (a - 1.0) * f64(k_a))
    return k_out, kk

@@ -1,0 +1,337 @@
+from contextlib import ExitStack
+
+import concourse.mybir as mybir
+from concourse.masks import make_identity
+
+F32 = mybir.dt.float32
+BF16 = mybir.dt.bfloat16
+U32 = mybir.dt.uint32
+U8 = mybir.dt.uint8
+FP8X4 = mybir.dt.float8_e4m3fn_x4
+ALU = mybir.AluOpType
+ACT = mybir.ActivationFunctionType
+
+P = 128
+PACK = 4
+B, T, C, CO, HS, DA = 4, 1024, 1024, 256, 64, 128
+PASSES = C // (P * PACK)
+CHUNKS = C // P
+CO_HALVES = CO // P
+UNIT = 512
+UNITS = B * T // UNIT
+UNITS_T = T // UNIT
+TILES_U = UNIT // P
+TILES = B * T // P
+STEPS_U = CHUNKS // 2
+STEPS = UNITS * STEPS_U
+GROUPS = UNITS * PASSES
+PAIRS = TILES // 2
+PAIRS_U = TILES_U // 2
+HEADS2 = 2 * CO // HS
+EPS_NORM = 1e-12
+
+FLOPS = 2 * B * T * C * CO + 2 * B * T * DA * CO
+
+
+def tile_full_tmix_params_pa_t_kernel(tc, x, x_k, W_k, a_hid, a2, a0, k_k, k_a, out_0, out_1):
+    nc = tc.nc
+    x_units = x.flatten_outer_dims().rearrange("(v n p) k -> v p n k", n=TILES_U, p=P)
+    a_rows = a_hid.flatten_outer_dims().rearrange("(n p) k -> p n k", p=P)
+    k_out_v = out_0.flatten_outer_dims().rearrange("(n p) c -> p n c", p=P)
+    kk_v = out_1.flatten_outer_dims().rearrange("(n p) c -> p n c", p=P)
+
+    with ExitStack() as ctx:
+        ctx.enter_context(tc.manual_schedule())
+        keep = ctx.enter_context(tc.tile_pool(name="keep", bufs=1))
+        work = ctx.enter_context(tc.tile_pool(name="work", bufs=2))
+        mx = ctx.enter_context(tc.tile_pool(name="mx", bufs=4))
+        tail = ctx.enter_context(tc.tile_pool(name="tail", bufs=3))
+        psum_t = ctx.enter_context(tc.psum_pool(name="psum_t", bufs=4))
+        psum_acc = ctx.enter_context(tc.psum_pool(name="psum_acc", bufs=4))
+
+        rows = keep.tile([P, P], BF16)
+        nc.vector.memset(rows[:], 0.0)
+        nc.sync.dma_start(out=rows[0:CHUNKS, :], in_=x_k.rearrange("a b (c p) -> (a b c) p", p=P))
+        nc.sync.dma_start(
+            out=rows[CHUNKS : CHUNKS + CO_HALVES, :], in_=a0.rearrange("a b (h p) -> (a b h) p", p=P)
+        )
+        a2_sb = keep.tile([P, CO], BF16)
+        nc.sync.dma_start(out=a2_sb[:], in_=a2)
+        a_sb = keep.tile([P, TILES, DA], BF16)
+        for q in range(B):
+            tiles_q = slice(TILES // B * q, TILES // B * (q + 1))
+            nc.sync.dma_start(out=a_sb[:, tiles_q, :], in_=a_rows[:, tiles_q, :])
+        w_sb = keep.tile([P, CO_HALVES, C], BF16)
+        nc.sync.dma_start(out=w_sb[:], in_=W_k.rearrange("(h p) k -> p h k", p=P))
+        x_sb = []
+        for v in range(UNITS):
+            x_v = keep.tile([P, TILES_U, C], BF16, name="x_sb%d" % v)
+            nc.sync.dma_start(out=x_v[:], in_=x_units[v])
+            x_sb.append(x_v)
+        ka_b = keep.tile([P, CO], BF16)
+        nc.scalar.dma_start(out=ka_b[:], in_=k_a.rearrange("a b c -> (a b c)").partition_broadcast(P))
+        kk_b = keep.tile([P, CO], BF16)
+        nc.scalar.dma_start(out=kk_b[:], in_=k_k.rearrange("a b c -> (a b c)").partition_broadcast(P))
+
+        ident = keep.tile([P, P], BF16)
+        make_identity(nc, ident[:])
+        ident_f32 = keep.tile([P, P], F32)
+        make_identity(nc, ident_f32[:])
+
+        u = []
+        for chunk in range(CHUNKS):
+            u_c = keep.tile([P, T + 1], F32, name="u%d" % chunk)
+            nc.vector.memset(u_c[:, 0:1], 0.0)
+            u.append(u_c)
+        eps2 = keep.tile([P, 1], F32)
+        nc.vector.memset(eps2[:], EPS_NORM * EPS_NORM)
+        neg_eps2 = keep.tile([P, 1], F32)
+        nc.vector.memset(neg_eps2[:], -EPS_NORM * EPS_NORM)
+
+        rows_ps = psum_t.tile([P, P], BF16, tag="t")
+        nc.tensor.transpose(out=rows_ps[:], in_=rows[:], identity=ident[:])
+        mix = keep.tile([P, CHUNKS], F32)
+        nc.vector.tensor_copy(out=mix[:], in_=rows_ps[:, 0:CHUNKS])
+        stay = keep.tile([P, CHUNKS], F32)
+        nc.vector.tensor_scalar(out=stay[:], in0=mix[:], scalar1=-1.0, scalar2=1.0, op0=ALU.mult, op1=ALU.add)
+        a0_cols = keep.tile([P, CO_HALVES, P], F32)
+        for h in range(CO_HALVES):
+            nc.vector.tensor_copy(
+                out=a0_cols[:, h, :], in_=rows_ps[:, CHUNKS + h : CHUNKS + h + 1].to_broadcast([P, P])
+            )
+
+        ahT = keep.tile([P, TILES, P], BF16)
+        gate1 = keep.tile([P, TILES, CO], F32)
+        TILES_Q = TILES // B
+
+        def transpose_a_hid(q):
+            ahT_ps = psum_t.tile([P, TILES_Q, P], BF16, tag="t")
+            for n in range(TILES_Q):
+                nc.tensor.transpose(out=ahT_ps[:, n, :], in_=a_sb[:, TILES_Q * q + n, :], identity=ident[:])
+            nc.scalar.copy(out=ahT[:, TILES_Q * q : TILES_Q * (q + 1), :], in_=ahT_ps[:])
+
+        def gate(pair):
+            z_ps = psum_acc.tile([P, 2, CO], F32, tag="acc")
+            for e in range(2):
+                for h in range(CO_HALVES):
+                    nc.tensor.matmul(
+                        out=z_ps[:, e, h * P : (h + 1) * P],
+                        lhsT=a0_cols[:, h, :],
+                        rhs=ident_f32[:],
+                        is_transpose=True,
+                        start=(h == 0),
+                        stop=False,
+                    )
+                nc.tensor.matmul(out=z_ps[:, e, :], lhsT=ahT[:, 2 * pair + e, :], rhs=a2_sb[:], start=False, stop=True)
+            a_gate = tail.tile([P, 2, CO], F32)
+            nc.scalar.activation(out=a_gate[:], in_=z_ps[:], func=ACT.Sigmoid)
+            nc.vector.scalar_tensor_tensor(
+                out=gate1[:, 2 * pair : 2 * pair + 2, :],
+                in0=a_gate[:],
+                scalar=1.0,
+                in1=ka_b[:].unsqueeze(1).to_broadcast([P, 2, CO]),
+                op0=ALU.subtract,
+                op1=ALU.mult,
+            )
+
+        transpose_a_hid(0)
+        for q in range(B):
+            if q + 1 < B:
+                transpose_a_hid(q + 1)
+            for pair in range(TILES_Q // 2 * q, TILES_Q // 2 * (q + 1)):
+                gate(pair)
+
+        w_codes = keep.tile([P, PASSES, CO], U32, align_bytes=64)
+        w_scales = keep.tile([P, PASSES, CO], U8, align_bytes=64)
+        for g in range(PASSES):
+            wT_ps = psum_t.tile([P, PACK, CO], BF16, tag="t")
+            for j in range(PACK):
+                for h in range(CO_HALVES):
+                    chunk = PACK * g + j
+                    nc.tensor.transpose(
+                        out=wT_ps[:, j, h * P : (h + 1) * P],
+                        in_=w_sb[:, h, chunk * P : (chunk + 1) * P],
+                        identity=ident[:],
+                    )
+            w_grouped = work.tile([P, CO, PACK], BF16, align_bytes=64)
+            nc.vector.tensor_copy(out=w_grouped[:], in_=wT_ps[:].rearrange("p j c -> p c j"))
+            nc.vector.quantize_mx(
+                out=w_codes[:, g, :].bitcast(FP8X4),
+                scales=w_scales[:, g, :],
+                in_=w_grouped[:].rearrange("p c j -> p (c j)"),
+            )
+
+        xT = {}
+        planes = {}
+        grouped = {}
+        codes = {}
+        scales = {}
+        k_ps = {}
+        kkh = {}
+        sumsq = {}
+        floored = {}
+        inv_norm = {}
+
+        def transpose_x(s):
+            v, pos = divmod(s, STEPS_U)
+            bank = psum_t.tile([P, 2, UNIT], BF16, tag="t")
+            for cc in range(2):
+                chunk = 2 * pos + cc
+                for n in range(TILES_U):
+                    nc.tensor.transpose(
+                        out=bank[:, cc, n * P : (n + 1) * P],
+                        in_=x_sb[v][:, n, chunk * P : (chunk + 1) * P],
+                        identity=ident[:],
+                    )
+            xT[s] = bank
+
+        def scale_prev(s):
+            v, pos = divmod(s, STEPS_U)
+            first = UNIT * (v % UNITS_T)
+            for cc in range(2):
+                chunk = 2 * pos + cc
+                nc.scalar.activation(
+                    out=u[chunk][:, first + 1 : first + 1 + UNIT],
+                    in_=xT[s][:, cc, :],
+                    func=ACT.Copy,
+                    scale=mix[:, chunk : chunk + 1],
+                )
+
+        def mix_tokens(s):
+            v, pos = divmod(s, STEPS_U)
+            first = UNIT * (v % UNITS_T)
+            i = s // 2
+            if s % 2 == 0:
+                new_planes = work.tile([P, PACK, UNIT], BF16, tag="planes")
+                planes[i] = new_planes
+            for cc in range(2):
+                chunk = 2 * pos + cc
+                nc.vector.scalar_tensor_tensor(
+                    out=planes[i][:, chunk % PACK, :],
+                    in0=xT[s][:, cc, :],
+                    scalar=stay[:, chunk : chunk + 1],
+                    in1=u[chunk][:, first : first + UNIT],
+                    op0=ALU.mult,
+                    op1=ALU.add,
+                )
+
+        def step(s):
+            if s + 3 < STEPS:
+                transpose_x(s + 3)
+            if s + 2 < STEPS:
+                scale_prev(s + 2)
+            if s < STEPS:
+                mix_tokens(s)
+
+        def regroup(i):
+            new_grouped = keep.tile([P, UNIT, PACK], BF16, align_bytes=64, tag="grouped")
+            nc.gpsimd.tensor_scalar(
+                out=new_grouped[:],
+                in0=planes[i][:].rearrange("p j r -> p r j"),
+                scalar1=1.0,
+                scalar2=0.0,
+                op0=ALU.mult,
+                op1=ALU.add,
+            )
+            grouped[i] = new_grouped
+
+        def quantise(i):
+            new_codes = mx.tile([P, UNIT], U32, align_bytes=64, tag="codes")
+            new_scales = mx.tile([P, UNIT], U8, align_bytes=64, tag="scales")
+            nc.vector.quantize_mx(
+                out=new_codes[:].bitcast(FP8X4),
+                scales=new_scales[:],
+                in_=grouped[i][:].rearrange("p r j -> p (r j)"),
+            )
+            codes[i] = new_codes
+            scales[i] = new_scales
+
+        def project(pair):
+            v, pos = divmod(pair, PAIRS_U)
+            acc = psum_acc.tile([P, 2, CO], F32, tag="acc")
+            for e in range(2):
+                tokens = slice((2 * pos + e) * P, (2 * pos + e + 1) * P)
+                for g in range(PASSES):
+                    nc.tensor.matmul_mx(
+                        out=acc[:, e, :],
+                        lhsT=codes[PASSES * v + g][:, tokens].bitcast(FP8X4),
+                        lhsT_scale=scales[PASSES * v + g][:, tokens],
+                        rhs=w_codes[:, g, :].bitcast(FP8X4),
+                        rhs_scale=w_scales[:, g, :],
+                        start=(g == 0),
+                        stop=(g == PASSES - 1),
+                    )
+            k_ps[pair] = acc
+
+        def scale_k(pair):
+            new_kkh = tail.tile([P, HEADS2, HS], F32, tag="kkh")
+            nc.vector.tensor_tensor(
+                out=new_kkh[:].rearrange("p (e h) d -> p e (h d)", e=2),
+                in0=k_ps[pair][:],
+                in1=kk_b[:].unsqueeze(1).to_broadcast([P, 2, CO]),
+                op=ALU.mult,
+            )
+            kkh[pair] = new_kkh
+            k_out_sb = tail.tile([P, 2, CO], F32)
+            nc.vector.scalar_tensor_tensor(
+                out=k_out_sb[:],
+                in0=gate1[:, 2 * pair : 2 * pair + 2, :],
+                scalar=1.0,
+                in1=k_ps[pair][:],
+                op0=ALU.add,
+                op1=ALU.mult,
+            )
+            nc.sync.dma_start(out=k_out_v[:, 2 * pair : 2 * pair + 2, :], in_=k_out_sb[:])
+
+        def sum_squares(pair):
+            squares = tail.tile([P, HEADS2, HS], F32)
+            new_sumsq = tail.tile([P, HEADS2], F32, tag="sumsq")
+            for h in range(HEADS2):
+                nc.scalar.activation(
+                    out=squares[:, h, :], in_=kkh[pair][:, h, :], func=ACT.Square, accum_out=new_sumsq[:, h : h + 1]
+                )
+            sumsq[pair] = new_sumsq
+
+        def floor_sum(pair):
+            new_floored = tail.tile([P, HEADS2], F32, tag="floored")
+            nc.scalar.activation(out=new_floored[:], in_=sumsq[pair][:], func=ACT.Relu, bias=neg_eps2[:])
+            floored[pair] = new_floored
+
+        def invert_norm(pair):
+            new_inv = tail.tile([P, HEADS2], F32, tag="inv_norm")
+            nc.scalar.activation(out=new_inv[:], in_=floored[pair][:], func=ACT.Abs_reciprocal_sqrt, bias=eps2[:])
+            inv_norm[pair] = new_inv
+
+        def divide(pair):
+            kk_sb = tail.tile([P, HEADS2, HS], F32)
+            for h in range(HEADS2):
+                nc.scalar.activation(
+                    out=kk_sb[:, h, :], in_=kkh[pair][:, h, :], func=ACT.Copy, scale=inv_norm[pair][:, h : h + 1]
+                )
+            nc.sync.dma_start(
+                out=kk_v[:, 2 * pair : 2 * pair + 2, :], in_=kk_sb[:].rearrange("p (e h) d -> p e (h d)", e=2)
+            )
+
+        for s in range(3):
+            transpose_x(s)
+        for s in range(2):
+            scale_prev(s)
+        for i in range(GROUPS + 5):
+            if 0 <= i - 4 < PAIRS:
+                sum_squares(i - 4)
+            step(2 * i)
+            if 0 <= i - 4 < PAIRS:
+                floor_sum(i - 4)
+            if 0 <= i - 5 < PAIRS:
+                divide(i - 5)
+            if 0 <= i - 4 < PAIRS:
+                invert_norm(i - 4)
+            step(2 * i + 1)
+            if 0 <= i - 3 < PAIRS:
+                scale_k(i - 3)
+            if 0 <= i - 1 < GROUPS:
+                quantise(i - 1)
+            if i < GROUPS:
+                regroup(i)
+            if 0 <= i - 2 < PAIRS:
+                project(i - 2)

@@ -28,6 +28,8 @@ GROUPS = UNITS * PASSES
 PAIRS = TILES // 2
 PAIRS_U = TILES_U // 2
 HEADS2 = 2 * CO // HS
+TILES_Q = 8
+QUARTERS = TILES // TILES_Q
 EPS_NORM = 1e-12
 
 FLOPS = 2 * B * T * C * CO + 2 * B * T * DA * CO
@@ -41,7 +43,6 @@ def tile_full_tmix_params_pa_t_kernel(tc, x, x_k, W_k, a_hid, a2, a0, k_k, k_a, 
     kk_v = out_1.flatten_outer_dims().rearrange("(n p) c -> p n c", p=P)
 
     with ExitStack() as ctx:
-        ctx.enter_context(tc.manual_schedule())
         keep = ctx.enter_context(tc.tile_pool(name="keep", bufs=1))
         work = ctx.enter_context(tc.tile_pool(name="work", bufs=2))
         mx = ctx.enter_context(tc.tile_pool(name="mx", bufs=4))
@@ -55,19 +56,20 @@ def tile_full_tmix_params_pa_t_kernel(tc, x, x_k, W_k, a_hid, a2, a0, k_k, k_a, 
         nc.sync.dma_start(
             out=rows[CHUNKS : CHUNKS + CO_HALVES, :], in_=a0.rearrange("a b (h p) -> (a b h) p", p=P)
         )
-        a2_sb = keep.tile([P, CO], BF16)
-        nc.sync.dma_start(out=a2_sb[:], in_=a2)
-        a_sb = keep.tile([P, TILES, DA], BF16)
-        for q in range(B):
-            tiles_q = slice(TILES // B * q, TILES // B * (q + 1))
-            nc.sync.dma_start(out=a_sb[:, tiles_q, :], in_=a_rows[:, tiles_q, :])
         w_sb = keep.tile([P, CO_HALVES, C], BF16)
         nc.sync.dma_start(out=w_sb[:], in_=W_k.rearrange("(h p) k -> p h k", p=P))
+        a2_sb = keep.tile([P, CO], BF16)
+        a_sb = keep.tile([P, TILES, DA], BF16)
         x_sb = []
         for v in range(UNITS):
             x_v = keep.tile([P, TILES_U, C], BF16, name="x_sb%d" % v)
             nc.sync.dma_start(out=x_v[:], in_=x_units[v])
             x_sb.append(x_v)
+            if v == 0:
+                nc.sync.dma_start(out=a2_sb[:], in_=a2)
+            if v < QUARTERS:
+                tiles_q = slice(TILES_Q * v, TILES_Q * (v + 1))
+                nc.sync.dma_start(out=a_sb[:, tiles_q, :], in_=a_rows[:, tiles_q, :])
         ka_b = keep.tile([P, CO], BF16)
         nc.scalar.dma_start(out=ka_b[:], in_=k_a.rearrange("a b c -> (a b c)").partition_broadcast(P))
         kk_b = keep.tile([P, CO], BF16)
@@ -100,12 +102,31 @@ def tile_full_tmix_params_pa_t_kernel(tc, x, x_k, W_k, a_hid, a2, a0, k_k, k_a, 
                 out=a0_cols[:, h, :], in_=rows_ps[:, CHUNKS + h : CHUNKS + h + 1].to_broadcast([P, P])
             )
 
+        w_codes = keep.tile([P, PASSES, CO], U32, align_bytes=64)
+        w_scales = keep.tile([P, PASSES, CO], U8, align_bytes=64)
+        for g in range(PASSES):
+            wT_ps = psum_acc.tile([P, PACK, CO], BF16, tag="acc")
+            for j in range(PACK):
+                for h in range(CO_HALVES):
+                    chunk = PACK * g + j
+                    nc.tensor.transpose(
+                        out=wT_ps[:, j, h * P : (h + 1) * P],
+                        in_=w_sb[:, h, chunk * P : (chunk + 1) * P],
+                        identity=ident[:],
+                    )
+            w_grouped = work.tile([P, CO, PACK], BF16, align_bytes=64)
+            nc.vector.tensor_copy(out=w_grouped[:], in_=wT_ps[:].rearrange("p j c -> p c j"))
+            nc.vector.quantize_mx(
+                out=w_codes[:, g, :].bitcast(FP8X4),
+                scales=w_scales[:, g, :],
+                in_=w_grouped[:].rearrange("p c j -> p (c j)"),
+            )
+
         ahT = keep.tile([P, TILES, P], BF16)
         gate1 = keep.tile([P, TILES, CO], F32)
-        TILES_Q = TILES // B
 
         def transpose_a_hid(q):
-            ahT_ps = psum_t.tile([P, TILES_Q, P], BF16, tag="t")
+            ahT_ps = psum_acc.tile([P, TILES_Q, P], BF16, tag="acc")
             for n in range(TILES_Q):
                 nc.tensor.transpose(out=ahT_ps[:, n, :], in_=a_sb[:, TILES_Q * q + n, :], identity=ident[:])
             nc.scalar.copy(out=ahT[:, TILES_Q * q : TILES_Q * (q + 1), :], in_=ahT_ps[:])
@@ -134,32 +155,9 @@ def tile_full_tmix_params_pa_t_kernel(tc, x, x_k, W_k, a_hid, a2, a0, k_k, k_a, 
                 op1=ALU.mult,
             )
 
-        transpose_a_hid(0)
-        for q in range(B):
-            if q + 1 < B:
-                transpose_a_hid(q + 1)
+        def gate_quarter(q):
             for pair in range(TILES_Q // 2 * q, TILES_Q // 2 * (q + 1)):
                 gate(pair)
-
-        w_codes = keep.tile([P, PASSES, CO], U32, align_bytes=64)
-        w_scales = keep.tile([P, PASSES, CO], U8, align_bytes=64)
-        for g in range(PASSES):
-            wT_ps = psum_t.tile([P, PACK, CO], BF16, tag="t")
-            for j in range(PACK):
-                for h in range(CO_HALVES):
-                    chunk = PACK * g + j
-                    nc.tensor.transpose(
-                        out=wT_ps[:, j, h * P : (h + 1) * P],
-                        in_=w_sb[:, h, chunk * P : (chunk + 1) * P],
-                        identity=ident[:],
-                    )
-            w_grouped = work.tile([P, CO, PACK], BF16, align_bytes=64)
-            nc.vector.tensor_copy(out=w_grouped[:], in_=wT_ps[:].rearrange("p j c -> p c j"))
-            nc.vector.quantize_mx(
-                out=w_codes[:, g, :].bitcast(FP8X4),
-                scales=w_scales[:, g, :],
-                in_=w_grouped[:].rearrange("p c j -> p (c j)"),
-            )
 
         xT = {}
         planes = {}
@@ -316,6 +314,7 @@ def tile_full_tmix_params_pa_t_kernel(tc, x, x_k, W_k, a_hid, a2, a0, k_k, k_a, 
             transpose_x(s)
         for s in range(2):
             scale_prev(s)
+        transpose_a_hid(0)
         for i in range(GROUPS + 5):
             if 0 <= i - 4 < PAIRS:
                 sum_squares(i - 4)
@@ -327,11 +326,15 @@ def tile_full_tmix_params_pa_t_kernel(tc, x, x_k, W_k, a_hid, a2, a0, k_k, k_a, 
             if 0 <= i - 4 < PAIRS:
                 invert_norm(i - 4)
             step(2 * i + 1)
-            if 0 <= i - 3 < PAIRS:
-                scale_k(i - 3)
             if 0 <= i - 1 < GROUPS:
                 quantise(i - 1)
             if i < GROUPS:
                 regroup(i)
+            if 0 <= i - 3 < PAIRS:
+                scale_k(i - 3)
+            if i < QUARTERS:
+                gate_quarter(i)
+            if i + 1 < QUARTERS:
+                transpose_a_hid(i + 1)
             if 0 <= i - 2 < PAIRS:
                 project(i - 2)

@@ -47,8 +47,8 @@ def tile_full_tmix_params_pa_t_kernel(tc, x, x_k, W_k, a_hid, a2, a0, k_k, k_a, 
         work = ctx.enter_context(tc.tile_pool(name="work", bufs=2))
         mx = ctx.enter_context(tc.tile_pool(name="mx", bufs=4))
         tail = ctx.enter_context(tc.tile_pool(name="tail", bufs=3))
-        psum_t = ctx.enter_context(tc.psum_pool(name="psum_t", bufs=4))
-        psum_acc = ctx.enter_context(tc.psum_pool(name="psum_acc", bufs=4))
+        psum_t = ctx.enter_context(tc.psum_pool(name="psum_t", bufs=6))
+        psum_acc = ctx.enter_context(tc.psum_pool(name="psum_acc", bufs=2))
 
         rows = keep.tile([P, P], BF16)
         nc.vector.memset(rows[:], 0.0)
@@ -105,17 +105,17 @@ def tile_full_tmix_params_pa_t_kernel(tc, x, x_k, W_k, a_hid, a2, a0, k_k, k_a, 
         w_codes = keep.tile([P, PASSES, CO], U32, align_bytes=64)
         w_scales = keep.tile([P, PASSES, CO], U8, align_bytes=64)
         for g in range(PASSES):
-            wT_ps = psum_acc.tile([P, PACK, CO], BF16, tag="acc")
-            for j in range(PACK):
-                for h in range(CO_HALVES):
+            w_grouped = work.tile([P, CO, PACK], BF16, align_bytes=64)
+            for h in range(CO_HALVES):
+                wT_ps = psum_acc.tile([P, PACK, P], BF16, tag="acc")
+                for j in range(PACK):
                     chunk = PACK * g + j
                     nc.tensor.transpose(
-                        out=wT_ps[:, j, h * P : (h + 1) * P],
-                        in_=w_sb[:, h, chunk * P : (chunk + 1) * P],
-                        identity=ident[:],
+                        out=wT_ps[:, j, :], in_=w_sb[:, h, chunk * P : (chunk + 1) * P], identity=ident[:]
                     )
-            w_grouped = work.tile([P, CO, PACK], BF16, align_bytes=64)
-            nc.vector.tensor_copy(out=w_grouped[:], in_=wT_ps[:].rearrange("p j c -> p c j"))
+                nc.vector.tensor_copy(
+                    out=w_grouped[:, h * P : (h + 1) * P, :], in_=wT_ps[:].rearrange("p j c -> p c j")
+                )
             nc.vector.quantize_mx(
                 out=w_codes[:, g, :].bitcast(FP8X4),
                 scales=w_scales[:, g, :],
@@ -126,10 +126,11 @@ def tile_full_tmix_params_pa_t_kernel(tc, x, x_k, W_k, a_hid, a2, a0, k_k, k_a, 
         gate1 = keep.tile([P, TILES, CO], F32)
 
         def transpose_a_hid(q):
-            ahT_ps = psum_acc.tile([P, TILES_Q, P], BF16, tag="acc")
-            for n in range(TILES_Q):
-                nc.tensor.transpose(out=ahT_ps[:, n, :], in_=a_sb[:, TILES_Q * q + n, :], identity=ident[:])
-            nc.scalar.copy(out=ahT[:, TILES_Q * q : TILES_Q * (q + 1), :], in_=ahT_ps[:])
+            for first in range(TILES_Q * q, TILES_Q * (q + 1), TILES_U):
+                ahT_ps = psum_acc.tile([P, TILES_U, P], BF16, tag="acc")
+                for n in range(TILES_U):
+                    nc.tensor.transpose(out=ahT_ps[:, n, :], in_=a_sb[:, first + n, :], identity=ident[:])
+                nc.scalar.copy(out=ahT[:, first : first + TILES_U, :], in_=ahT_ps[:])
 
         def gate(pair):
             z_ps = psum_acc.tile([P, 2, CO], F32, tag="acc")
@@ -172,16 +173,17 @@ def tile_full_tmix_params_pa_t_kernel(tc, x, x_k, W_k, a_hid, a2, a0, k_k, k_a, 
 
         def transpose_x(s):
             v, pos = divmod(s, STEPS_U)
-            bank = psum_t.tile([P, 2, UNIT], BF16, tag="t")
+            xT[s] = []
             for cc in range(2):
                 chunk = 2 * pos + cc
+                bank = psum_t.tile([P, UNIT], BF16, tag="t")
                 for n in range(TILES_U):
                     nc.tensor.transpose(
-                        out=bank[:, cc, n * P : (n + 1) * P],
+                        out=bank[:, n * P : (n + 1) * P],
                         in_=x_sb[v][:, n, chunk * P : (chunk + 1) * P],
                         identity=ident[:],
                     )
-            xT[s] = bank
+                xT[s].append(bank)
 
         def scale_prev(s):
             v, pos = divmod(s, STEPS_U)
@@ -190,7 +192,7 @@ def tile_full_tmix_params_pa_t_kernel(tc, x, x_k, W_k, a_hid, a2, a0, k_k, k_a, 
                 chunk = 2 * pos + cc
                 nc.scalar.activation(
                     out=u[chunk][:, first + 1 : first + 1 + UNIT],
-                    in_=xT[s][:, cc, :],
+                    in_=xT[s][cc][:],
                     func=ACT.Copy,
                     scale=mix[:, chunk : chunk + 1],
                 )
@@ -206,7 +208,7 @@ def tile_full_tmix_params_pa_t_kernel(tc, x, x_k, W_k, a_hid, a2, a0, k_k, k_a, 
                 chunk = 2 * pos + cc
                 nc.vector.scalar_tensor_tensor(
                     out=planes[i][:, chunk % PACK, :],
-                    in0=xT[s][:, cc, :],
+                    in0=xT[s][cc][:],
                     scalar=stay[:, chunk : chunk + 1],
                     in1=u[chunk][:, first : first + UNIT],
                     op0=ALU.mult,
@@ -214,10 +216,10 @@ def tile_full_tmix_params_pa_t_kernel(tc, x, x_k, W_k, a_hid, a2, a0, k_k, k_a, 
                 )
 
         def step(s):
-            if s + 3 < STEPS:
-                transpose_x(s + 3)
             if s + 2 < STEPS:
-                scale_prev(s + 2)
+                transpose_x(s + 2)
+            if s + 1 < STEPS:
+                scale_prev(s + 1)
             if s < STEPS:
                 mix_tokens(s)
 
@@ -310,10 +312,9 @@ def tile_full_tmix_params_pa_t_kernel(tc, x, x_k, W_k, a_hid, a2, a0, k_k, k_a, 
                 out=kk_v[:, 2 * pair : 2 * pair + 2, :], in_=kk_sb[:].rearrange("p (e h) d -> p e (h d)", e=2)
             )
 
-        for s in range(3):
-            transpose_x(s)
         for s in range(2):
-            scale_prev(s)
+            transpose_x(s)
+        scale_prev(0)
         transpose_a_hid(0)
         for i in range(GROUPS + 5):
             if 0 <= i - 4 < PAIRS:

@@ -15,14 +15,14 @@ P = 128
 PACK = 4
 B, T, C, CO, HS, DA = 4, 1024, 1024, 256, 64, 128
 PASSES = C // (P * PACK)
-CHUNKS = C // P
+PLANES = C // P
 CO_HALVES = CO // P
 UNIT = 512
 UNITS = B * T // UNIT
 UNITS_T = T // UNIT
 TILES_U = UNIT // P
 TILES = B * T // P
-STEPS_U = CHUNKS // 2
+STEPS_U = PLANES // 2
 STEPS = UNITS * STEPS_U
 GROUPS = UNITS * PASSES
 PAIRS = TILES // 2
@@ -47,15 +47,19 @@ def tile_full_tmix_params_pa_t_kernel(tc, x, x_k, W_k, a_hid, a2, a0, k_k, k_a, 
         work = ctx.enter_context(tc.tile_pool(name="work", bufs=2))
         mx = ctx.enter_context(tc.tile_pool(name="mx", bufs=4))
         tail = ctx.enter_context(tc.tile_pool(name="tail", bufs=3))
-        psum_t = ctx.enter_context(tc.psum_pool(name="psum_t", bufs=6))
-        psum_acc = ctx.enter_context(tc.psum_pool(name="psum_acc", bufs=2))
+        psum_t = ctx.enter_context(tc.psum_pool(name="psum_t", bufs=4))
+        psum_acc = ctx.enter_context(tc.psum_pool(name="psum_acc", bufs=4))
 
-        rows = keep.tile([P, P], BF16)
-        nc.vector.memset(rows[:], 0.0)
-        nc.sync.dma_start(out=rows[0:CHUNKS, :], in_=x_k.rearrange("a b (c p) -> (a b c) p", p=P))
-        nc.sync.dma_start(
-            out=rows[CHUNKS : CHUNKS + CO_HALVES, :], in_=a0.rearrange("a b (h p) -> (a b h) p", p=P)
-        )
+        xk_rows = keep.tile([P, 2 * P], BF16)
+        nc.vector.memset(xk_rows[:], 0.0)
+        nc.sync.dma_start(out=xk_rows[0:STEPS_U, :], in_=x_k.rearrange("a b (s c) -> (a b s) c", s=STEPS_U))
+        co_rows = keep.tile([P, P], BF16)
+        nc.vector.memset(co_rows[:], 0.0)
+        for n, vector_co in enumerate((a0, k_a, k_k)):
+            nc.sync.dma_start(
+                out=co_rows[CO_HALVES * n : CO_HALVES * (n + 1), :],
+                in_=vector_co.rearrange("a b (h p) -> (a b h) p", p=P),
+            )
         w_sb = keep.tile([P, CO_HALVES, C], BF16)
         nc.sync.dma_start(out=w_sb[:], in_=W_k.rearrange("(h p) k -> p h k", p=P))
         a2_sb = keep.tile([P, CO], BF16)
@@ -70,10 +74,6 @@ def tile_full_tmix_params_pa_t_kernel(tc, x, x_k, W_k, a_hid, a2, a0, k_k, k_a, 
             if v < QUARTERS:
                 tiles_q = slice(TILES_Q * v, TILES_Q * (v + 1))
                 nc.sync.dma_start(out=a_sb[:, tiles_q, :], in_=a_rows[:, tiles_q, :])
-        ka_b = keep.tile([P, CO], BF16)
-        nc.scalar.dma_start(out=ka_b[:], in_=k_a.rearrange("a b c -> (a b c)").partition_broadcast(P))
-        kk_b = keep.tile([P, CO], BF16)
-        nc.scalar.dma_start(out=kk_b[:], in_=k_k.rearrange("a b c -> (a b c)").partition_broadcast(P))
 
         ident = keep.tile([P, P], BF16)
         make_identity(nc, ident[:])
@@ -81,8 +81,8 @@ def tile_full_tmix_params_pa_t_kernel(tc, x, x_k, W_k, a_hid, a2, a0, k_k, k_a, 
         make_identity(nc, ident_f32[:])
 
         u = []
-        for chunk in range(CHUNKS):
-            u_c = keep.tile([P, T + 1], F32, name="u%d" % chunk)
+        for plane in range(PLANES):
+            u_c = keep.tile([P, T + 1], F32, name="u%d" % plane)
             nc.vector.memset(u_c[:, 0:1], 0.0)
             u.append(u_c)
         eps2 = keep.tile([P, 1], F32)
@@ -90,47 +90,59 @@ def tile_full_tmix_params_pa_t_kernel(tc, x, x_k, W_k, a_hid, a2, a0, k_k, k_a, 
         neg_eps2 = keep.tile([P, 1], F32)
         nc.vector.memset(neg_eps2[:], -EPS_NORM * EPS_NORM)
 
-        rows_ps = psum_t.tile([P, P], BF16, tag="t")
-        nc.tensor.transpose(out=rows_ps[:], in_=rows[:], identity=ident[:])
-        mix = keep.tile([P, CHUNKS], F32)
-        nc.vector.tensor_copy(out=mix[:], in_=rows_ps[:, 0:CHUNKS])
-        stay = keep.tile([P, CHUNKS], F32)
+        xk_ps = psum_t.tile([P, P], F32, tag="t")
+        nc.tensor.transpose(out=xk_ps[:], in_=xk_rows[:].bitcast(F32), identity=ident_f32[:])
+        mix = keep.tile([P, PLANES], F32)
+        nc.vector.tensor_copy(out=mix[:], in_=xk_ps[:, 0:STEPS_U].bitcast(BF16))
+        stay = keep.tile([P, PLANES], F32)
         nc.vector.tensor_scalar(out=stay[:], in0=mix[:], scalar1=-1.0, scalar2=1.0, op0=ALU.mult, op1=ALU.add)
-        a0_cols = keep.tile([P, CO_HALVES, P], F32)
-        for h in range(CO_HALVES):
-            nc.vector.tensor_copy(
-                out=a0_cols[:, h, :], in_=rows_ps[:, CHUNKS + h : CHUNKS + h + 1].to_broadcast([P, P])
-            )
+        co_ps = psum_t.tile([P, P], BF16, tag="t")
+        nc.tensor.transpose(out=co_ps[:], in_=co_rows[:], identity=ident[:])
+        cols = keep.tile([P, 3, CO_HALVES, P], F32)
+        nc.vector.tensor_copy(
+            out=cols[:].rearrange("p n h t -> p (n h) t"),
+            in_=co_ps[:, 0 : 3 * CO_HALVES].unsqueeze(2).to_broadcast([P, 3 * CO_HALVES, P]),
+        )
+        a0_cols = cols[:, 0, :, :]
+        spread_ps = psum_acc.tile([P, 2, CO], F32, tag="acc")
+        for n in range(2):
+            for h in range(CO_HALVES):
+                nc.tensor.transpose(
+                    out=spread_ps[:, n, h * P : (h + 1) * P], in_=cols[:, n + 1, h, :], identity=ident_f32[:]
+                )
+        neg_ka_b = keep.tile([P, CO], F32)
+        nc.vector.tensor_scalar_mul(out=neg_ka_b[:], in0=spread_ps[:, 0, :], scalar1=-1.0)
+        kk_b = keep.tile([P, CO], F32)
+        nc.vector.tensor_copy(out=kk_b[:], in_=spread_ps[:, 1, :])
 
         w_codes = keep.tile([P, PASSES, CO], U32, align_bytes=64)
         w_scales = keep.tile([P, PASSES, CO], U8, align_bytes=64)
         for g in range(PASSES):
-            w_grouped = work.tile([P, CO, PACK], BF16, align_bytes=64)
-            for h in range(CO_HALVES):
-                wT_ps = psum_acc.tile([P, PACK, P], BF16, tag="acc")
-                for j in range(PACK):
-                    chunk = PACK * g + j
+            wT_ps = psum_acc.tile([P, 2, CO], F32, tag="acc")
+            for w in range(2):
+                for h in range(CO_HALVES):
+                    block = 2 * g + w
                     nc.tensor.transpose(
-                        out=wT_ps[:, j, :], in_=w_sb[:, h, chunk * P : (chunk + 1) * P], identity=ident[:]
+                        out=wT_ps[:, w, h * P : (h + 1) * P],
+                        in_=w_sb[:, h, :].bitcast(F32)[:, block * P : (block + 1) * P],
+                        identity=ident_f32[:],
                     )
-                nc.vector.tensor_copy(
-                    out=w_grouped[:, h * P : (h + 1) * P, :], in_=wT_ps[:].rearrange("p j c -> p c j")
-                )
+            w_grouped = work.tile([P, CO, 2], F32, align_bytes=64)
+            nc.vector.tensor_copy(out=w_grouped[:], in_=wT_ps[:].rearrange("p w c -> p c w"))
             nc.vector.quantize_mx(
                 out=w_codes[:, g, :].bitcast(FP8X4),
                 scales=w_scales[:, g, :],
-                in_=w_grouped[:].rearrange("p c j -> p (c j)"),
+                in_=w_grouped[:].rearrange("p c w -> p (c w)").bitcast(BF16),
             )
 
         ahT = keep.tile([P, TILES, P], BF16)
         gate1 = keep.tile([P, TILES, CO], F32)
 
         def transpose_a_hid(q):
-            for first in range(TILES_Q * q, TILES_Q * (q + 1), TILES_U):
-                ahT_ps = psum_acc.tile([P, TILES_U, P], BF16, tag="acc")
-                for n in range(TILES_U):
-                    nc.tensor.transpose(out=ahT_ps[:, n, :], in_=a_sb[:, first + n, :], identity=ident[:])
-                nc.scalar.copy(out=ahT[:, first : first + TILES_U, :], in_=ahT_ps[:])
+            ahT_ps = psum_acc.tile([P, TILES_Q, P], BF16, tag="acc")
+            for n in range(TILES_Q):
+                nc.tensor.transpose(out=ahT_ps[:, n, :], in_=a_sb[:, TILES_Q * q + n, :], identity=ident[:])
+            nc.vector.tensor_copy(out=ahT[:, TILES_Q * q : TILES_Q * (q + 1), :], in_=ahT_ps[:])
 
         def gate(pair):
             z_ps = psum_acc.tile([P, 2, CO], F32, tag="acc")
@@ -145,15 +157,14 @@ def tile_full_tmix_params_pa_t_kernel(tc, x, x_k, W_k, a_hid, a2, a0, k_k, k_a, 
                         stop=False,
                     )
                 nc.tensor.matmul(out=z_ps[:, e, :], lhsT=ahT[:, 2 * pair + e, :], rhs=a2_sb[:], start=False, stop=True)
-            a_gate = tail.tile([P, 2, CO], F32)
-            nc.scalar.activation(out=a_gate[:], in_=z_ps[:], func=ACT.Sigmoid)
-            nc.vector.scalar_tensor_tensor(
+            one_minus_a = tail.tile([P, 2, CO], F32)
+            nc.scalar.activation(out=one_minus_a[:], in_=z_ps[:], func=ACT.Sigmoid, scale=-1.0)
+            engine = nc.vector if pair % 2 == 0 else nc.gpsimd
+            engine.tensor_tensor(
                 out=gate1[:, 2 * pair : 2 * pair + 2, :],
-                in0=a_gate[:],
-                scalar=1.0,
-                in1=ka_b[:].unsqueeze(1).to_broadcast([P, 2, CO]),
-                op0=ALU.subtract,
-                op1=ALU.mult,
+                in0=one_minus_a[:],
+                in1=neg_ka_b[:].unsqueeze(1).to_broadcast([P, 2, CO]),
+                op=ALU.mult,
             )
 
         def gate_quarter(q):
@@ -172,54 +183,51 @@ def tile_full_tmix_params_pa_t_kernel(tc, x, x_k, W_k, a_hid, a2, a0, k_k, k_a, 
         inv_norm = {}
 
         def transpose_x(s):
-            v, pos = divmod(s, STEPS_U)
-            xT[s] = []
-            for cc in range(2):
-                chunk = 2 * pos + cc
-                bank = psum_t.tile([P, UNIT], BF16, tag="t")
-                for n in range(TILES_U):
-                    nc.tensor.transpose(
-                        out=bank[:, n * P : (n + 1) * P],
-                        in_=x_sb[v][:, n, chunk * P : (chunk + 1) * P],
-                        identity=ident[:],
-                    )
-                xT[s].append(bank)
+            v, block = divmod(s, STEPS_U)
+            bank = psum_t.tile([P, UNIT], F32, tag="t")
+            for n in range(TILES_U):
+                nc.tensor.transpose(
+                    out=bank[:, n * P : (n + 1) * P],
+                    in_=x_sb[v][:, n, :].bitcast(F32)[:, block * P : (block + 1) * P],
+                    identity=ident_f32[:],
+                )
+            xT[s] = bank[:].bitcast(BF16).rearrange("p (r e) -> p r e", e=2)
 
         def scale_prev(s):
-            v, pos = divmod(s, STEPS_U)
+            v, block = divmod(s, STEPS_U)
             first = UNIT * (v % UNITS_T)
-            for cc in range(2):
-                chunk = 2 * pos + cc
+            for e in range(2):
+                plane = 2 * block + e
                 nc.scalar.activation(
-                    out=u[chunk][:, first + 1 : first + 1 + UNIT],
-                    in_=xT[s][cc][:],
+                    out=u[plane][:, first + 1 : first + 1 + UNIT],
+                    in_=xT[s][:, :, e],
                     func=ACT.Copy,
-                    scale=mix[:, chunk : chunk + 1],
+                    scale=mix[:, plane : plane + 1],
                 )
 
         def mix_tokens(s):
-            v, pos = divmod(s, STEPS_U)
+            v, block = divmod(s, STEPS_U)
             first = UNIT * (v % UNITS_T)
             i = s // 2
             if s % 2 == 0:
                 new_planes = work.tile([P, PACK, UNIT], BF16, tag="planes")
                 planes[i] = new_planes
-            for cc in range(2):
-                chunk = 2 * pos + cc
+            for e in range(2):
+                plane = 2 * block + e
                 nc.vector.scalar_tensor_tensor(
-                    out=planes[i][:, chunk % PACK, :],
-                    in0=xT[s][cc][:],
-                    scalar=stay[:, chunk : chunk + 1],
-                    in1=u[chunk][:, first : first + UNIT],
+                    out=planes[i][:, plane % PACK, :],
+                    in0=xT[s][:, :, e],
+                    scalar=stay[:, plane : plane + 1],
+                    in1=u[plane][:, first : first + UNIT],
                     op0=ALU.mult,
                     op1=ALU.add,
                 )
 
         def step(s):
+            if s + 3 < STEPS:
+                transpose_x(s + 3)
             if s + 2 < STEPS:
-                transpose_x(s + 2)
-            if s + 1 < STEPS:
-                scale_prev(s + 1)
+                scale_prev(s + 2)
             if s < STEPS:
                 mix_tokens(s)
 
@@ -304,17 +312,26 @@ def tile_full_tmix_params_pa_t_kernel(tc, x, x_k, W_k, a_hid, a2, a0, k_k, k_a, 
 
         def divide(pair):
             kk_sb = tail.tile([P, HEADS2, HS], F32)
-            for h in range(HEADS2):
-                nc.scalar.activation(
-                    out=kk_sb[:, h, :], in_=kkh[pair][:, h, :], func=ACT.Copy, scale=inv_norm[pair][:, h : h + 1]
+            if pair % 2 == 0:
+                for h in range(HEADS2):
+                    nc.scalar.activation(
+                        out=kk_sb[:, h, :], in_=kkh[pair][:, h, :], func=ACT.Copy, scale=inv_norm[pair][:, h : h + 1]
+                    )
+            else:
+                nc.gpsimd.tensor_tensor(
+                    out=kk_sb[:],
+                    in0=kkh[pair][:],
+                    in1=inv_norm[pair][:].unsqueeze(2).to_broadcast([P, HEADS2, HS]),
+                    op=ALU.mult,
                 )
             nc.sync.dma_start(
                 out=kk_v[:, 2 * pair : 2 * pair + 2, :], in_=kk_sb[:].rearrange("p (e h) d -> p e (h d)", e=2)
             )
 
-        for s in range(2):
+        for s in range(3):
             transpose_x(s)
-        scale_prev(0)
+        for s in range(2):
+            scale_prev(s)
         transpose_a_hid(0)
         for i in range(GROUPS + 5):
             if 0 <= i - 4 < PAIRS:

from contextlib import ExitStack

import concourse.mybir as mybir
from concourse.masks import make_identity

F32 = mybir.dt.float32
BF16 = mybir.dt.bfloat16
U32 = mybir.dt.uint32
U8 = mybir.dt.uint8
FP8X4 = mybir.dt.float8_e4m3fn_x4
ALU = mybir.AluOpType
ACT = mybir.ActivationFunctionType

P = 128
PACK = 4
B, T, C, CO, HS, DA = 4, 1024, 1024, 256, 64, 128
PASSES = C // (P * PACK)
PLANES = C // P
CO_HALVES = CO // P
UNIT = 512
UNITS = B * T // UNIT
UNITS_T = T // UNIT
TILES_U = UNIT // P
TILES = B * T // P
STEPS_U = PLANES // 2
STEPS = UNITS * STEPS_U
GROUPS = UNITS * PASSES
PAIRS = TILES // 2
PAIRS_U = TILES_U // 2
HEADS2 = 2 * CO // HS
TILES_Q = 8
QUARTERS = TILES // TILES_Q
EPS_NORM = 1e-12

FLOPS = 2 * B * T * C * CO + 2 * B * T * DA * CO


def tile_full_tmix_params_pa_t_kernel(tc, x, x_k, W_k, a_hid, a2, a0, k_k, k_a, out_0, out_1):
    nc = tc.nc
    x_units = x.flatten_outer_dims().rearrange("(v n p) k -> v p n k", n=TILES_U, p=P)
    a_rows = a_hid.flatten_outer_dims().rearrange("(n p) k -> p n k", p=P)
    k_out_v = out_0.flatten_outer_dims().rearrange("(n p) c -> p n c", p=P)
    kk_v = out_1.flatten_outer_dims().rearrange("(n p) c -> p n c", p=P)

    with ExitStack() as ctx:
        keep = ctx.enter_context(tc.tile_pool(name="keep", bufs=1))
        work = ctx.enter_context(tc.tile_pool(name="work", bufs=2))
        mx = ctx.enter_context(tc.tile_pool(name="mx", bufs=4))
        tail = ctx.enter_context(tc.tile_pool(name="tail", bufs=3))
        psum_t = ctx.enter_context(tc.psum_pool(name="psum_t", bufs=4))
        psum_acc = ctx.enter_context(tc.psum_pool(name="psum_acc", bufs=4))

        xk_rows = keep.tile([P, 2 * P], BF16)
        nc.vector.memset(xk_rows[:], 0.0)
        nc.sync.dma_start(out=xk_rows[0:STEPS_U, :], in_=x_k.rearrange("a b (s c) -> (a b s) c", s=STEPS_U))
        co_rows = keep.tile([P, P], BF16)
        nc.vector.memset(co_rows[:], 0.0)
        for n, vector_co in enumerate((a0, k_a, k_k)):
            nc.sync.dma_start(
                out=co_rows[CO_HALVES * n : CO_HALVES * (n + 1), :],
                in_=vector_co.rearrange("a b (h p) -> (a b h) p", p=P),
            )
        w_sb = keep.tile([P, CO_HALVES, C], BF16)
        nc.sync.dma_start(out=w_sb[:], in_=W_k.rearrange("(h p) k -> p h k", p=P))
        a2_sb = keep.tile([P, CO], BF16)
        a_sb = keep.tile([P, TILES, DA], BF16)
        x_sb = []
        for v in range(UNITS):
            x_v = keep.tile([P, TILES_U, C], BF16, name="x_sb%d" % v)
            nc.sync.dma_start(out=x_v[:], in_=x_units[v])
            x_sb.append(x_v)
            if v == 0:
                nc.sync.dma_start(out=a2_sb[:], in_=a2)
            if v < QUARTERS:
                tiles_q = slice(TILES_Q * v, TILES_Q * (v + 1))
                nc.sync.dma_start(out=a_sb[:, tiles_q, :], in_=a_rows[:, tiles_q, :])

        ident = keep.tile([P, P], BF16)
        make_identity(nc, ident[:])
        ident_f32 = keep.tile([P, P], F32)
        make_identity(nc, ident_f32[:])

        u = []
        for plane in range(PLANES):
            u_c = keep.tile([P, T + 1], F32, name="u%d" % plane)
            nc.vector.memset(u_c[:, 0:1], 0.0)
            u.append(u_c)
        eps2 = keep.tile([P, 1], F32)
        nc.vector.memset(eps2[:], EPS_NORM * EPS_NORM)
        neg_eps2 = keep.tile([P, 1], F32)
        nc.vector.memset(neg_eps2[:], -EPS_NORM * EPS_NORM)

        xk_ps = psum_t.tile([P, P], F32, tag="t")
        nc.tensor.transpose(out=xk_ps[:], in_=xk_rows[:].bitcast(F32), identity=ident_f32[:])
        mix = keep.tile([P, PLANES], F32)
        nc.vector.tensor_copy(out=mix[:], in_=xk_ps[:, 0:STEPS_U].bitcast(BF16))
        stay = keep.tile([P, PLANES], F32)
        nc.vector.tensor_scalar(out=stay[:], in0=mix[:], scalar1=-1.0, scalar2=1.0, op0=ALU.mult, op1=ALU.add)
        co_ps = psum_t.tile([P, P], BF16, tag="t")
        nc.tensor.transpose(out=co_ps[:], in_=co_rows[:], identity=ident[:])
        cols = keep.tile([P, 3, CO_HALVES, P], F32)
        nc.vector.tensor_copy(
            out=cols[:].rearrange("p n h t -> p (n h) t"),
            in_=co_ps[:, 0 : 3 * CO_HALVES].unsqueeze(2).to_broadcast([P, 3 * CO_HALVES, P]),
        )
        a0_cols = cols[:, 0, :, :]
        spread_ps = psum_acc.tile([P, 2, CO], F32, tag="acc")
        for n in range(2):
            for h in range(CO_HALVES):
                nc.tensor.transpose(
                    out=spread_ps[:, n, h * P : (h + 1) * P], in_=cols[:, n + 1, h, :], identity=ident_f32[:]
                )
        neg_ka_b = keep.tile([P, CO], F32)
        nc.vector.tensor_scalar_mul(out=neg_ka_b[:], in0=spread_ps[:, 0, :], scalar1=-1.0)
        kk_b = keep.tile([P, CO], F32)
        nc.vector.tensor_copy(out=kk_b[:], in_=spread_ps[:, 1, :])

        w_codes = keep.tile([P, PASSES, CO], U32, align_bytes=64)
        w_scales = keep.tile([P, PASSES, CO], U8, align_bytes=64)
        for g in range(PASSES):
            wT_ps = psum_acc.tile([P, 2, CO], F32, tag="acc")
            for w in range(2):
                for h in range(CO_HALVES):
                    block = 2 * g + w
                    nc.tensor.transpose(
                        out=wT_ps[:, w, h * P : (h + 1) * P],
                        in_=w_sb[:, h, :].bitcast(F32)[:, block * P : (block + 1) * P],
                        identity=ident_f32[:],
                    )
            w_grouped = work.tile([P, CO, 2], F32, align_bytes=64)
            nc.vector.tensor_copy(out=w_grouped[:], in_=wT_ps[:].rearrange("p w c -> p c w"))
            nc.vector.quantize_mx(
                out=w_codes[:, g, :].bitcast(FP8X4),
                scales=w_scales[:, g, :],
                in_=w_grouped[:].rearrange("p c w -> p (c w)").bitcast(BF16),
            )

        ahT = keep.tile([P, TILES, P], BF16)
        gate1 = keep.tile([P, TILES, CO], F32)

        def transpose_a_hid(q):
            ahT_ps = psum_acc.tile([P, TILES_Q, P], BF16, tag="acc")
            for n in range(TILES_Q):
                nc.tensor.transpose(out=ahT_ps[:, n, :], in_=a_sb[:, TILES_Q * q + n, :], identity=ident[:])
            nc.vector.tensor_copy(out=ahT[:, TILES_Q * q : TILES_Q * (q + 1), :], in_=ahT_ps[:])

        def gate(pair):
            z_ps = psum_acc.tile([P, 2, CO], F32, tag="acc")
            for e in range(2):
                for h in range(CO_HALVES):
                    nc.tensor.matmul(
                        out=z_ps[:, e, h * P : (h + 1) * P],
                        lhsT=a0_cols[:, h, :],
                        rhs=ident_f32[:],
                        is_transpose=True,
                        start=(h == 0),
                        stop=False,
                    )
                nc.tensor.matmul(out=z_ps[:, e, :], lhsT=ahT[:, 2 * pair + e, :], rhs=a2_sb[:], start=False, stop=True)
            one_minus_a = tail.tile([P, 2, CO], F32)
            nc.scalar.activation(out=one_minus_a[:], in_=z_ps[:], func=ACT.Sigmoid, scale=-1.0)
            engine = nc.vector if pair % 2 == 0 else nc.gpsimd
            engine.tensor_tensor(
                out=gate1[:, 2 * pair : 2 * pair + 2, :],
                in0=one_minus_a[:],
                in1=neg_ka_b[:].unsqueeze(1).to_broadcast([P, 2, CO]),
                op=ALU.mult,
            )

        def gate_quarter(q):
            for pair in range(TILES_Q // 2 * q, TILES_Q // 2 * (q + 1)):
                gate(pair)

        xT = {}
        planes = {}
        grouped = {}
        codes = {}
        scales = {}
        k_ps = {}
        kkh = {}
        sumsq = {}
        floored = {}
        inv_norm = {}

        def transpose_x(s):
            v, block = divmod(s, STEPS_U)
            bank = psum_t.tile([P, UNIT], F32, tag="t")
            for n in range(TILES_U):
                nc.tensor.transpose(
                    out=bank[:, n * P : (n + 1) * P],
                    in_=x_sb[v][:, n, :].bitcast(F32)[:, block * P : (block + 1) * P],
                    identity=ident_f32[:],
                )
            xT[s] = bank[:].bitcast(BF16).rearrange("p (r e) -> p r e", e=2)

        def scale_prev(s):
            v, block = divmod(s, STEPS_U)
            first = UNIT * (v % UNITS_T)
            for e in range(2):
                plane = 2 * block + e
                nc.scalar.activation(
                    out=u[plane][:, first + 1 : first + 1 + UNIT],
                    in_=xT[s][:, :, e],
                    func=ACT.Copy,
                    scale=mix[:, plane : plane + 1],
                )

        def mix_tokens(s):
            v, block = divmod(s, STEPS_U)
            first = UNIT * (v % UNITS_T)
            i = s // 2
            if s % 2 == 0:
                new_planes = work.tile([P, PACK, UNIT], BF16, tag="planes")
                planes[i] = new_planes
            for e in range(2):
                plane = 2 * block + e
                nc.vector.scalar_tensor_tensor(
                    out=planes[i][:, plane % PACK, :],
                    in0=xT[s][:, :, e],
                    scalar=stay[:, plane : plane + 1],
                    in1=u[plane][:, first : first + UNIT],
                    op0=ALU.mult,
                    op1=ALU.add,
                )

        def step(s):
            if s + 3 < STEPS:
                transpose_x(s + 3)
            if s + 2 < STEPS:
                scale_prev(s + 2)
            if s < STEPS:
                mix_tokens(s)

        def regroup(i):
            new_grouped = keep.tile([P, UNIT, PACK], BF16, align_bytes=64, tag="grouped")
            nc.gpsimd.tensor_scalar(
                out=new_grouped[:],
                in0=planes[i][:].rearrange("p j r -> p r j"),
                scalar1=1.0,
                scalar2=0.0,
                op0=ALU.mult,
                op1=ALU.add,
            )
            grouped[i] = new_grouped

        def quantise(i):
            new_codes = mx.tile([P, UNIT], U32, align_bytes=64, tag="codes")
            new_scales = mx.tile([P, UNIT], U8, align_bytes=64, tag="scales")
            nc.vector.quantize_mx(
                out=new_codes[:].bitcast(FP8X4),
                scales=new_scales[:],
                in_=grouped[i][:].rearrange("p r j -> p (r j)"),
            )
            codes[i] = new_codes
            scales[i] = new_scales

        def project(pair):
            v, pos = divmod(pair, PAIRS_U)
            acc = psum_acc.tile([P, 2, CO], F32, tag="acc")
            for e in range(2):
                tokens = slice((2 * pos + e) * P, (2 * pos + e + 1) * P)
                for g in range(PASSES):
                    nc.tensor.matmul_mx(
                        out=acc[:, e, :],
                        lhsT=codes[PASSES * v + g][:, tokens].bitcast(FP8X4),
                        lhsT_scale=scales[PASSES * v + g][:, tokens],
                        rhs=w_codes[:, g, :].bitcast(FP8X4),
                        rhs_scale=w_scales[:, g, :],
                        start=(g == 0),
                        stop=(g == PASSES - 1),
                    )
            k_ps[pair] = acc

        def scale_k(pair):
            new_kkh = tail.tile([P, HEADS2, HS], F32, tag="kkh")
            nc.vector.tensor_tensor(
                out=new_kkh[:].rearrange("p (e h) d -> p e (h d)", e=2),
                in0=k_ps[pair][:],
                in1=kk_b[:].unsqueeze(1).to_broadcast([P, 2, CO]),
                op=ALU.mult,
            )
            kkh[pair] = new_kkh
            k_out_sb = tail.tile([P, 2, CO], F32)
            nc.vector.scalar_tensor_tensor(
                out=k_out_sb[:],
                in0=gate1[:, 2 * pair : 2 * pair + 2, :],
                scalar=1.0,
                in1=k_ps[pair][:],
                op0=ALU.add,
                op1=ALU.mult,
            )
            nc.sync.dma_start(out=k_out_v[:, 2 * pair : 2 * pair + 2, :], in_=k_out_sb[:])

        def sum_squares(pair):
            squares = tail.tile([P, HEADS2, HS], F32)
            new_sumsq = tail.tile([P, HEADS2], F32, tag="sumsq")
            for h in range(HEADS2):
                nc.scalar.activation(
                    out=squares[:, h, :], in_=kkh[pair][:, h, :], func=ACT.Square, accum_out=new_sumsq[:, h : h + 1]
                )
            sumsq[pair] = new_sumsq

        def floor_sum(pair):
            new_floored = tail.tile([P, HEADS2], F32, tag="floored")
            nc.scalar.activation(out=new_floored[:], in_=sumsq[pair][:], func=ACT.Relu, bias=neg_eps2[:])
            floored[pair] = new_floored

        def invert_norm(pair):
            new_inv = tail.tile([P, HEADS2], F32, tag="inv_norm")
            nc.scalar.activation(out=new_inv[:], in_=floored[pair][:], func=ACT.Abs_reciprocal_sqrt, bias=eps2[:])
            inv_norm[pair] = new_inv

        def divide(pair):
            kk_sb = tail.tile([P, HEADS2, HS], F32)
            if pair % 2 == 0:
                for h in range(HEADS2):
                    nc.scalar.activation(
                        out=kk_sb[:, h, :], in_=kkh[pair][:, h, :], func=ACT.Copy, scale=inv_norm[pair][:, h : h + 1]
                    )
            else:
                nc.gpsimd.tensor_tensor(
                    out=kk_sb[:],
                    in0=kkh[pair][:],
                    in1=inv_norm[pair][:].unsqueeze(2).to_broadcast([P, HEADS2, HS]),
                    op=ALU.mult,
                )
            nc.sync.dma_start(
                out=kk_v[:, 2 * pair : 2 * pair + 2, :], in_=kk_sb[:].rearrange("p (e h) d -> p e (h d)", e=2)
            )

        for s in range(3):
            transpose_x(s)
        for s in range(2):
            scale_prev(s)
        transpose_a_hid(0)
        for i in range(GROUPS + 5):
            if 0 <= i - 4 < PAIRS:
                sum_squares(i - 4)
            step(2 * i)
            if 0 <= i - 4 < PAIRS:
                floor_sum(i - 4)
            if 0 <= i - 5 < PAIRS:
                divide(i - 5)
            if 0 <= i - 4 < PAIRS:
                invert_norm(i - 4)
            step(2 * i + 1)
            if 0 <= i - 1 < GROUPS:
                quantise(i - 1)
            if i < GROUPS:
                regroup(i)
            if 0 <= i - 3 < PAIRS:
                scale_k(i - 3)
            if i < QUARTERS:
                gate_quarter(i)
            if i + 1 < QUARTERS:
                transpose_a_hid(i + 1)
            if 0 <= i - 2 < PAIRS:
                project(i - 2)
